import numpy as np
import ml_dtypes


def mxq(x, axis, fmt="e4m3"):
    dtype, down = {"e4m3": (ml_dtypes.float8_e4m3fn, 7), "e5m2": (ml_dtypes.float8_e5m2, 14)}[fmt]
    v = np.moveaxis(np.asarray(x, np.float32).astype(ml_dtypes.bfloat16).astype(np.float64), axis, -1)
    blocks = v.reshape(v.shape[:-1] + (-1, 32))
    amax = np.abs(blocks).max(-1, keepdims=True)
    byte = np.maximum(np.where(amax > 0, np.frexp(amax)[1] - 1 + 127, 0) - down, 1)
    scale = np.exp2(byte - 127.0)
    codes = (blocks / scale).astype(np.float32).astype(dtype).astype(np.float64)
    return np.moveaxis((codes * scale).reshape(v.shape), -1, axis)


WIDE = False


def mx_kscale(k):
    if not WIDE:
        return np.ones(k)
    levels = np.array([10, -10, 5, -5, 0])
    a = np.random.permutation(np.resize(levels, k // 512 * 4)).reshape(k // 512, 4)
    idx = np.arange(k)
    return np.exp2(a[idx // 512, idx % 128 // 32])


BF16 = ml_dtypes.bfloat16


def bf(x):
    return np.asarray(x, np.float32).astype(BF16)


def f64(x):
    return np.asarray(x).astype(np.float64)


T, B, F, H, R, O = 1024, 8, 1024, 1024, 512, 128


def setup_inputs():
    s, t = mx_kscale(R), mx_kscale(H)
    return {"z2": bf(np.random.standard_normal((T, B, R)) * s),
            "sw1": bf(np.random.standard_normal((R, H)) / np.sqrt(R) / s[:, None] * t),
            "b2": bf(np.random.standard_normal((B, H)) * t),
            "w3": bf(np.random.standard_normal((B, H, O)) / np.sqrt(H) / t[:, None]),
            "b3": bf(np.random.standard_normal((B, O)))}


def reference(z2, sw1, b2, w3, b3):
    u = (mxq(f64(z2), 2, "e4m3").reshape(T * B, R) @ mxq(f64(sw1), 0, "e4m3")).reshape(T, B, H)
    h = np.maximum(u + f64(b2)[None, :, :], 0.0)
    out = (mxq(h, 2, "e4m3").transpose(1, 0, 2) @ mxq(f64(w3), 1, "e4m3")) + f64(b3)[:, None, :]
    return out.transpose(1, 0, 2)

@@ -1,0 +1,287 @@
+from contextlib import ExitStack
+
+import concourse.mybir as mybir
+from concourse.masks import make_identity
+
+F32 = mybir.dt.float32
+BF16 = mybir.dt.bfloat16
+U32 = mybir.dt.uint32
+U8 = mybir.dt.uint8
+FP8X4 = mybir.dt.float8_e4m3fn_x4
+RELU = mybir.ActivationFunctionType.Relu
+ADD = mybir.AluOpType.add
+
+T, B, R, H, O = 1024, 8, 512, 1024, 128
+P = 128
+PACK = 4
+UNIT = 512
+UNITS_PER_DATASET = T // UNIT
+UNITS = B * UNITS_PER_DATASET
+TOKEN_TILES = UNIT // P
+CHUNKS = H // P
+GROUPS = CHUNKS // PACK
+HALF = UNIT // 2
+AHEAD = 3
+SCALAR_BOTH = 2
+
+FLOPS = 2 * T * B * R * H + 2 * T * B * H * O
+
+
+def regroup(nc, grouped, planes):
+    nc.vector.tensor_copy(
+        out=grouped.rearrange("p (c i) t -> p c t i", i=4),
+        in_=planes.rearrange("p t (c i) -> p c t i", i=4),
+    )
+
+
+def quantise(nc, codes, scales, grouped):
+    nc.vector.quantize_mx(
+        out=codes.bitcast(FP8X4),
+        scales=scales,
+        in_=grouped.rearrange("p c t -> p (c t)"),
+    )
+
+
+def tile_mlpmodelpredictor_pb_t_kernel(tc, z2, sw1, b2, w3, b3, out):
+    nc = tc.nc
+    with ExitStack() as stack:
+        keep = stack.enter_context(tc.tile_pool(name="keep", bufs=1))
+        z_raw_pool = stack.enter_context(tc.tile_pool(name="z_raw", bufs=AHEAD + 1))
+        w_pool = stack.enter_context(tc.tile_pool(name="w3", bufs=2))
+        z_pool = stack.enter_context(tc.tile_pool(name="z", bufs=2))
+        plane_pool = stack.enter_context(tc.tile_pool(name="planes", bufs=3))
+        h_pool = stack.enter_context(tc.tile_pool(name="h", bufs=2))
+        h_mx_pool = stack.enter_context(tc.tile_pool(name="h_mx", bufs=4))
+        out_pool = stack.enter_context(tc.tile_pool(name="out", bufs=3))
+        psum_z = stack.enter_context(tc.psum_pool(name="psum_z", bufs=1))
+        psum_u = stack.enter_context(tc.psum_pool(name="psum_u", bufs=4))
+        psum_o = stack.enter_context(tc.psum_pool(name="psum_o", bufs=2))
+
+        z_raw = {}
+        z_banks = {}
+        z_grouped = {}
+        z_mx = {}
+        planes = {}
+        h_grouped = {}
+        h_mx = {}
+        w_raw = {}
+        w_grouped = {}
+        w_mx = {}
+        o_banks = {}
+
+        def load_z(n):
+            b, s = divmod(n, UNITS_PER_DATASET)
+            rows = z_raw_pool.tile([P, TOKEN_TILES, R], BF16, name="z_rows")
+            nc.sync.dma_start(
+                out=rows[:],
+                in_=z2[s * UNIT : (s + 1) * UNIT, b, :].rearrange("(j p) r -> p j r", p=P),
+            )
+            z_raw[n] = rows
+
+        def load_w(b):
+            rows = w_pool.tile([P, CHUNKS, O], BF16, name="w_rows")
+            nc.sync.dma_start(out=rows[:], in_=w3[b].rearrange("(c p) o -> p c o", p=P))
+            w_raw[b] = rows
+
+        def transpose_z(n):
+            words = z_raw[n][:].bitcast(F32)
+            for half in range(2):
+                bank = psum_z.tile([P, 2, HALF], F32, name="z_bank%d" % half)
+                for u in range(2):
+                    for i in range(HALF // P):
+                        j = half * (HALF // P) + i
+                        nc.tensor.transpose(
+                            out=bank[:, u, i * P : (i + 1) * P],
+                            in_=words[:, j, u * P : (u + 1) * P],
+                            identity=ident[:],
+                        )
+                z_banks[n, half] = bank
+
+        def copy_z(n, half):
+            if half == 0:
+                z_grouped[n] = z_pool.tile([P, UNIT, PACK], BF16, name="z_grouped", align_bytes=64)
+            on_scalar = half == 0 or n % SCALAR_BOTH == SCALAR_BOTH - 1
+            copy = nc.scalar.copy if on_scalar else nc.vector.tensor_copy
+            copy(
+                out=z_grouped[n][:].bitcast(F32)[:, half * HALF : (half + 1) * HALF, :],
+                in_=z_banks[n, half][:].rearrange("p u r -> p r u"),
+            )
+
+        def quantise_z(n):
+            codes = z_pool.tile([P, UNIT], U32, name="z_codes", align_bytes=64)
+            scales = z_pool.tile([P, UNIT], U8, name="z_scales", align_bytes=64)
+            quantise(nc, codes[:], scales[:], z_grouped[n][:])
+            z_mx[n] = (codes, scales)
+
+        def hidden(n, g):
+            b = n // UNITS_PER_DATASET
+            z_codes, z_scales = z_mx[n]
+            four = plane_pool.tile([P, PACK, UNIT], BF16, name="planes")
+            for t in range(PACK):
+                c = g * PACK + t
+                cols = slice(c * P, (c + 1) * P)
+                u_bank = psum_u.tile([P, UNIT], F32, name="u_bank")
+                nc.tensor.matmul_mx(
+                    out=u_bank[:],
+                    lhsT=s_codes[:, cols].bitcast(FP8X4),
+                    lhsT_scale=s_scales[:, cols],
+                    rhs=z_codes[:].bitcast(FP8X4),
+                    rhs_scale=z_scales[:],
+                    start=True,
+                    stop=True,
+                )
+                nc.scalar.activation(
+                    out=four[:, t, :],
+                    in_=u_bank[:],
+                    func=RELU,
+                    bias=b2_cols[:, b * CHUNKS + c : b * CHUNKS + c + 1],
+                    scale=1.0,
+                )
+            planes[n, g] = four
+
+        def regroup_h(n, g):
+            grouped = h_pool.tile([P, UNIT, PACK], BF16, name="h_grouped", align_bytes=64)
+            regroup(nc, grouped[:], planes[n, g][:])
+            h_grouped[n, g] = grouped
+
+        def quantise_h(n, g):
+            codes = h_mx_pool.tile([P, UNIT], U32, name="h_codes", align_bytes=64)
+            scales = h_mx_pool.tile([P, UNIT], U8, name="h_scales", align_bytes=64)
+            quantise(nc, codes[:], scales[:], h_grouped[n, g][:])
+            h_mx[n, g] = (codes, scales)
+
+        def regroup_w(b):
+            grouped = w_pool.tile([P, GROUPS * O, PACK], BF16, name="w_grouped", align_bytes=64)
+            for g in range(GROUPS):
+                regroup(
+                    nc,
+                    grouped[:, g * O : (g + 1) * O, :],
+                    w_raw[b][:, g * PACK : (g + 1) * PACK, :],
+                )
+            w_grouped[b] = grouped
+
+        def quantise_w(b):
+            codes = w_pool.tile([P, GROUPS * O], U32, name="w_codes", align_bytes=64)
+            scales = w_pool.tile([P, GROUPS * O], U8, name="w_scales", align_bytes=64)
+            quantise(nc, codes[:], scales[:], w_grouped[b][:])
+            w_mx[b] = (codes, scales)
+
+        def output(n):
+            w_codes, w_scales = w_mx[n // UNITS_PER_DATASET]
+            o_bank = psum_o.tile([P, TOKEN_TILES, O], F32, name="o_bank")
+            for j in range(TOKEN_TILES):
+                tokens = slice(j * P, (j + 1) * P)
+                for g in range(GROUPS):
+                    h_codes, h_scales = h_mx[n, g]
+                    w_cols = slice(g * O, (g + 1) * O)
+                    nc.tensor.matmul_mx(
+                        out=o_bank[:, j, :],
+                        lhsT=h_codes[:, tokens].bitcast(FP8X4),
+                        lhsT_scale=h_scales[:, tokens],
+                        rhs=w_codes[:, w_cols].bitcast(FP8X4),
+                        rhs_scale=w_scales[:, w_cols],
+                        start=(g == 0),
+                        stop=(g == GROUPS - 1),
+                    )
+            o_banks[n] = o_bank
+
+        def store(n):
+            b, s = divmod(n, UNITS_PER_DATASET)
+            result = out_pool.tile([P, TOKEN_TILES, O], F32, name="result")
+            nc.vector.tensor_tensor(
+                out=result[:],
+                in0=o_banks[n][:],
+                in1=b3_all[:, b, :].unsqueeze(1).to_broadcast([P, TOKEN_TILES, O]),
+                op=ADD,
+            )
+            nc.sync.dma_start(
+                out=out[s * UNIT : (s + 1) * UNIT, b, :].rearrange("(j p) o -> p j o", p=P),
+                in_=result[:],
+            )
+
+        s_rows = keep.tile([P, 2, PACK, UNIT], BF16, name="s_rows")
+        for col_half in range(2):
+            for u in range(2):
+                nc.sync.dma_start(
+                    out=s_rows[:, col_half, 2 * u : 2 * u + 2, :],
+                    in_=sw1[
+                        256 * u : 256 * (u + 1), col_half * UNIT : (col_half + 1) * UNIT
+                    ].rearrange("(q e) c -> q e c", e=2),
+                )
+            if col_half == 0:
+                load_z(0)
+        b2_rows = keep.tile([P, P], BF16, name="b2_rows")
+        nc.vector.memset(b2_rows[:], 0.0)
+        nc.sync.dma_start(
+            out=b2_rows[0 : B * CHUNKS, :], in_=b2.rearrange("b (c p) -> (b c) p", p=P)
+        )
+        load_z(1)
+        load_w(0)
+        b3_all = keep.tile([P, B, O], BF16, name="b3_all")
+        nc.sync.dma_start(
+            out=b3_all[:].rearrange("p b o -> p (b o)"),
+            in_=b3.rearrange("b o -> (b o)").partition_broadcast(P),
+        )
+        load_z(2)
+
+        ident = keep.tile([P, P], F32, name="ident")
+        make_identity(nc, ident[:])
+
+        s_grouped = keep.tile([P, 2, UNIT, PACK], BF16, name="s_grouped", align_bytes=64)
+        s_codes = keep.tile([P, H], U32, name="s_codes", align_bytes=64)
+        s_scales = keep.tile([P, H], U8, name="s_scales", align_bytes=64)
+
+        def regroup_s(col_half):
+            regroup(nc, s_grouped[:, col_half], s_rows[:, col_half])
+
+        def quantise_s(col_half):
+            cols = slice(col_half * UNIT, (col_half + 1) * UNIT)
+            quantise(nc, s_codes[:, cols], s_scales[:, cols], s_grouped[:, col_half])
+
+        regroup_s(0)
+        transpose_z(0)
+        copy_z(0, 0)
+        copy_z(0, 1)
+        quantise_s(0)
+        regroup_s(1)
+        quantise_z(0)
+
+        b2_rows_f32 = keep.tile([P, P], F32, name="b2_rows_f32")
+        nc.vector.tensor_copy(out=b2_rows_f32[:], in_=b2_rows[:])
+        b2_bank = psum_o.tile([P, TOKEN_TILES, O], F32, name="o_bank")
+        nc.tensor.transpose(out=b2_bank[:, 0, :], in_=b2_rows_f32[:], identity=ident[:])
+        b2_cols = keep.tile([P, B * CHUNKS], F32, name="b2_cols")
+        nc.vector.tensor_copy(out=b2_cols[:], in_=b2_bank[:, 0, 0 : B * CHUNKS])
+        quantise_s(1)
+
+        for n in range(UNITS + 1):
+            if n + AHEAD < UNITS:
+                load_z(n + AHEAD)
+            if n % UNITS_PER_DATASET == 0 and n // UNITS_PER_DATASET + 1 < B:
+                load_w(n // UNITS_PER_DATASET + 1)
+            if n >= 1:
+                regroup_h(n - 1, 1)
+            if n < UNITS:
+                hidden(n, 0)
+            if n + 1 < UNITS:
+                transpose_z(n + 1)
+                copy_z(n + 1, 0)
+                copy_z(n + 1, 1)
+            if n >= 1:
+                quantise_h(n - 1, 1)
+            if n < UNITS:
+                hidden(n, 1)
+            if n >= 1:
+                output(n - 1)
+            if n < UNITS:
+                regroup_h(n, 0)
+            if n < UNITS and n % UNITS_PER_DATASET == 0:
+                regroup_w(n // UNITS_PER_DATASET)
+            if n + 1 < UNITS:
+                quantise_z(n + 1)
+            if n < UNITS:
+                quantise_h(n, 0)
+            if n < UNITS and n % UNITS_PER_DATASET == 0:
+                quantise_w(n // UNITS_PER_DATASET)
+            if n >= 1:
+                store(n - 1)

@@ -21,14 +21,14 @@ TOKEN_TILES = UNIT // P
 CHUNKS = H // P
 GROUPS = CHUNKS // PACK
 HALF = UNIT // 2
-AHEAD = 3
+AHEAD = 4
 SCALAR_BOTH = 2
 
 FLOPS = 2 * T * B * R * H + 2 * T * B * H * O
 
 
-def regroup(nc, grouped, planes):
-    nc.vector.tensor_copy(
+def regroup(copy, grouped, planes):
+    copy(
         out=grouped.rearrange("p (c i) t -> p c t i", i=4),
         in_=planes.rearrange("p t (c i) -> p c t i", i=4),
     )
@@ -46,7 +46,7 @@ def tile_mlpmodelpredictor_pb_t_kernel(tc, z2, sw1, b2, w3, b3, out):
     nc = tc.nc
     with ExitStack() as stack:
         keep = stack.enter_context(tc.tile_pool(name="keep", bufs=1))
-        z_raw_pool = stack.enter_context(tc.tile_pool(name="z_raw", bufs=AHEAD + 1))
+        z_raw_pool = stack.enter_context(tc.tile_pool(name="z_raw", bufs=AHEAD))
         w_pool = stack.enter_context(tc.tile_pool(name="w3", bufs=2))
         z_pool = stack.enter_context(tc.tile_pool(name="z", bufs=2))
         plane_pool = stack.enter_context(tc.tile_pool(name="planes", bufs=3))
@@ -56,6 +56,7 @@ def tile_mlpmodelpredictor_pb_t_kernel(tc, z2, sw1, b2, w3, b3, out):
         psum_z = stack.enter_context(tc.psum_pool(name="psum_z", bufs=1))
         psum_u = stack.enter_context(tc.psum_pool(name="psum_u", bufs=4))
         psum_o = stack.enter_context(tc.psum_pool(name="psum_o", bufs=2))
+        stack.enter_context(tc.manual_schedule())
 
         z_raw = {}
         z_banks = {}
@@ -97,11 +98,9 @@ def tile_mlpmodelpredictor_pb_t_kernel(tc, z2, sw1, b2, w3, b3, out):
                         )
                 z_banks[n, half] = bank
 
-        def copy_z(n, half):
+        def copy_z(n, half, copy):
             if half == 0:
                 z_grouped[n] = z_pool.tile([P, UNIT, PACK], BF16, name="z_grouped", align_bytes=64)
-            on_scalar = half == 0 or n % SCALAR_BOTH == SCALAR_BOTH - 1
-            copy = nc.scalar.copy if on_scalar else nc.vector.tensor_copy
             copy(
                 out=z_grouped[n][:].bitcast(F32)[:, half * HALF : (half + 1) * HALF, :],
                 in_=z_banks[n, half][:].rearrange("p u r -> p r u"),
@@ -141,7 +140,7 @@ def tile_mlpmodelpredictor_pb_t_kernel(tc, z2, sw1, b2, w3, b3, out):
 
         def regroup_h(n, g):
             grouped = h_pool.tile([P, UNIT, PACK], BF16, name="h_grouped", align_bytes=64)
-            regroup(nc, grouped[:], planes[n, g][:])
+            regroup(nc.vector.tensor_copy, grouped[:], planes[n, g][:])
             h_grouped[n, g] = grouped
 
         def quantise_h(n, g):
@@ -154,7 +153,7 @@ def tile_mlpmodelpredictor_pb_t_kernel(tc, z2, sw1, b2, w3, b3, out):
             grouped = w_pool.tile([P, GROUPS * O, PACK], BF16, name="w_grouped", align_bytes=64)
             for g in range(GROUPS):
                 regroup(
-                    nc,
+                    nc.vector.tensor_copy,
                     grouped[:, g * O : (g + 1) * O, :],
                     w_raw[b][:, g * PACK : (g + 1) * PACK, :],
                 )
@@ -200,7 +199,11 @@ def tile_mlpmodelpredictor_pb_t_kernel(tc, z2, sw1, b2, w3, b3, out):
             )
 
         s_rows = keep.tile([P, 2, PACK, UNIT], BF16, name="s_rows")
-        for col_half in range(2):
+        b2_rows = keep.tile([P, P], BF16, name="b2_rows")
+        b3_all = keep.tile([P, B, O], BF16, name="b3_all")
+        nc.vector.memset(b2_rows[:], 0.0)
+
+        def load_s(col_half):
             for u in range(2):
                 nc.sync.dma_start(
                     out=s_rows[:, col_half, 2 * u : 2 * u + 2, :],
@@ -208,21 +211,21 @@ def tile_mlpmodelpredictor_pb_t_kernel(tc, z2, sw1, b2, w3, b3, out):
                         256 * u : 256 * (u + 1), col_half * UNIT : (col_half + 1) * UNIT
                     ].rearrange("(q e) c -> q e c", e=2),
                 )
-            if col_half == 0:
-                load_z(0)
-        b2_rows = keep.tile([P, P], BF16, name="b2_rows")
-        nc.vector.memset(b2_rows[:], 0.0)
+
+        load_s(0)
+        load_z(0)
         nc.sync.dma_start(
             out=b2_rows[0 : B * CHUNKS, :], in_=b2.rearrange("b (c p) -> (b c) p", p=P)
         )
         load_z(1)
+        load_s(1)
         load_w(0)
-        b3_all = keep.tile([P, B, O], BF16, name="b3_all")
+        load_z(2)
         nc.sync.dma_start(
             out=b3_all[:].rearrange("p b o -> p (b o)"),
             in_=b3.rearrange("b o -> (b o)").partition_broadcast(P),
         )
-        load_z(2)
+        load_z(3)
 
         ident = keep.tile([P, P], F32, name="ident")
         make_identity(nc, ident[:])
@@ -232,7 +235,7 @@ def tile_mlpmodelpredictor_pb_t_kernel(tc, z2, sw1, b2, w3, b3, out):
         s_scales = keep.tile([P, H], U8, name="s_scales", align_bytes=64)
 
         def regroup_s(col_half):
-            regroup(nc, s_grouped[:, col_half], s_rows[:, col_half])
+            regroup(nc.vector.tensor_copy, s_grouped[:, col_half], s_rows[:, col_half])
 
         def quantise_s(col_half):
             cols = slice(col_half * UNIT, (col_half + 1) * UNIT)
@@ -240,10 +243,9 @@ def tile_mlpmodelpredictor_pb_t_kernel(tc, z2, sw1, b2, w3, b3, out):
 
         regroup_s(0)
         transpose_z(0)
-        copy_z(0, 0)
-        copy_z(0, 1)
         quantise_s(0)
-        regroup_s(1)
+        copy_z(0, 0, nc.scalar.copy)
+        copy_z(0, 1, nc.vector.tensor_copy)
         quantise_z(0)
 
         b2_rows_f32 = keep.tile([P, P], F32, name="b2_rows_f32")
@@ -252,36 +254,42 @@ def tile_mlpmodelpredictor_pb_t_kernel(tc, z2, sw1, b2, w3, b3, out):
         nc.tensor.transpose(out=b2_bank[:, 0, :], in_=b2_rows_f32[:], identity=ident[:])
         b2_cols = keep.tile([P, B * CHUNKS], F32, name="b2_cols")
         nc.vector.tensor_copy(out=b2_cols[:], in_=b2_bank[:, 0, 0 : B * CHUNKS])
+        transpose_z(1)
+        regroup_s(1)
+        copy_z(1, 0, nc.vector.tensor_copy)
         quantise_s(1)
+        copy_z(1, 1, nc.vector.tensor_copy)
 
-        for n in range(UNITS + 1):
+        for n in range(UNITS + 2):
+            b, first_of_dataset = n // UNITS_PER_DATASET, n % UNITS_PER_DATASET == 0
             if n + AHEAD < UNITS:
                 load_z(n + AHEAD)
-            if n % UNITS_PER_DATASET == 0 and n // UNITS_PER_DATASET + 1 < B:
-                load_w(n // UNITS_PER_DATASET + 1)
-            if n >= 1:
+            if first_of_dataset and b + 1 < B:
+                load_w(b + 1)
+            if 1 <= n <= UNITS:
                 regroup_h(n - 1, 1)
-            if n < UNITS:
-                hidden(n, 0)
-            if n + 1 < UNITS:
-                transpose_z(n + 1)
-                copy_z(n + 1, 0)
-                copy_z(n + 1, 1)
-            if n >= 1:
-                quantise_h(n - 1, 1)
-            if n < UNITS:
-                hidden(n, 1)
-            if n >= 1:
-                output(n - 1)
-            if n < UNITS:
-                regroup_h(n, 0)
-            if n < UNITS and n % UNITS_PER_DATASET == 0:
-                regroup_w(n // UNITS_PER_DATASET)
             if n + 1 < UNITS:
                 quantise_z(n + 1)
             if n < UNITS:
+                hidden(n, 0)
+            if 1 <= n <= UNITS:
+                quantise_h(n - 1, 1)
+            if n + 2 < UNITS:
+                both_on_scalar = n % SCALAR_BOTH == SCALAR_BOTH - 1
+                transpose_z(n + 2)
+                copy_z(n + 2, 0, nc.scalar.copy)
+                copy_z(n + 2, 1, nc.scalar.copy if both_on_scalar else nc.vector.tensor_copy)
+            if n < UNITS:
+                hidden(n, 1)
+            if 1 <= n <= UNITS:
+                output(n - 1)
+            if n < UNITS:
+                regroup_h(n, 0)
+                if first_of_dataset:
+                    regroup_w(b)
+            if n >= 2:
+                store(n - 2)
+            if n < UNITS:
                 quantise_h(n, 0)
-            if n < UNITS and n % UNITS_PER_DATASET == 0:
-                quantise_w(n // UNITS_PER_DATASET)
-            if n >= 1:
-                store(n - 1)
+                if first_of_dataset:
+                    quantise_w(b)

@@ -22,7 +22,7 @@ CHUNKS = H // P
 GROUPS = CHUNKS // PACK
 HALF = UNIT // 2
 AHEAD = 4
-SCALAR_BOTH = 2
+VECTOR_EVERY = 3
 
 FLOPS = 2 * T * B * R * H + 2 * T * B * H * O
 
@@ -212,15 +212,15 @@ def tile_mlpmodelpredictor_pb_t_kernel(tc, z2, sw1, b2, w3, b3, out):
                     ].rearrange("(q e) c -> q e c", e=2),
                 )
 
-        load_s(0)
-        load_z(0)
         nc.sync.dma_start(
             out=b2_rows[0 : B * CHUNKS, :], in_=b2.rearrange("b (c p) -> (b c) p", p=P)
         )
+        load_s(0)
+        load_z(0)
         load_z(1)
         load_s(1)
-        load_w(0)
         load_z(2)
+        load_w(0)
         nc.sync.dma_start(
             out=b3_all[:].rearrange("p b o -> p (b o)"),
             in_=b3.rearrange("b o -> (b o)").partition_broadcast(P),
@@ -241,19 +241,19 @@ def tile_mlpmodelpredictor_pb_t_kernel(tc, z2, sw1, b2, w3, b3, out):
             cols = slice(col_half * UNIT, (col_half + 1) * UNIT)
             quantise(nc, s_codes[:, cols], s_scales[:, cols], s_grouped[:, col_half])
 
-        regroup_s(0)
-        transpose_z(0)
-        quantise_s(0)
-        copy_z(0, 0, nc.scalar.copy)
-        copy_z(0, 1, nc.vector.tensor_copy)
-        quantise_z(0)
-
         b2_rows_f32 = keep.tile([P, P], F32, name="b2_rows_f32")
         nc.vector.tensor_copy(out=b2_rows_f32[:], in_=b2_rows[:])
         b2_bank = psum_o.tile([P, TOKEN_TILES, O], F32, name="o_bank")
         nc.tensor.transpose(out=b2_bank[:, 0, :], in_=b2_rows_f32[:], identity=ident[:])
         b2_cols = keep.tile([P, B * CHUNKS], F32, name="b2_cols")
         nc.vector.tensor_copy(out=b2_cols[:], in_=b2_bank[:, 0, 0 : B * CHUNKS])
+
+        regroup_s(0)
+        transpose_z(0)
+        quantise_s(0)
+        copy_z(0, 0, nc.scalar.copy)
+        copy_z(0, 1, nc.vector.tensor_copy)
+        quantise_z(0)
         transpose_z(1)
         regroup_s(1)
         copy_z(1, 0, nc.vector.tensor_copy)
@@ -275,10 +275,10 @@ def tile_mlpmodelpredictor_pb_t_kernel(tc, z2, sw1, b2, w3, b3, out):
             if 1 <= n <= UNITS:
                 quantise_h(n - 1, 1)
             if n + 2 < UNITS:
-                both_on_scalar = n % SCALAR_BOTH == SCALAR_BOTH - 1
+                vector_helps = n % VECTOR_EVERY == 0
                 transpose_z(n + 2)
                 copy_z(n + 2, 0, nc.scalar.copy)
-                copy_z(n + 2, 1, nc.scalar.copy if both_on_scalar else nc.vector.tensor_copy)
+                copy_z(n + 2, 1, nc.vector.tensor_copy if vector_helps else nc.scalar.copy)
             if n < UNITS:
                 hidden(n, 1)
             if 1 <= n <= UNITS:

@@ -21,14 +21,14 @@ TOKEN_TILES = UNIT // P
 CHUNKS = H // P
 GROUPS = CHUNKS // PACK
 HALF = UNIT // 2
+PAIR = 2
 AHEAD = 4
-VECTOR_EVERY = 3
 
 FLOPS = 2 * T * B * R * H + 2 * T * B * H * O
 
 
-def regroup(copy, grouped, planes):
-    copy(
+def regroup(nc, grouped, planes):
+    nc.vector.tensor_copy(
         out=grouped.rearrange("p (c i) t -> p c t i", i=4),
         in_=planes.rearrange("p t (c i) -> p c t i", i=4),
     )
@@ -51,7 +51,7 @@ def tile_mlpmodelpredictor_pb_t_kernel(tc, z2, sw1, b2, w3, b3, out):
         z_pool = stack.enter_context(tc.tile_pool(name="z", bufs=2))
         plane_pool = stack.enter_context(tc.tile_pool(name="planes", bufs=3))
         h_pool = stack.enter_context(tc.tile_pool(name="h", bufs=2))
-        h_mx_pool = stack.enter_context(tc.tile_pool(name="h_mx", bufs=4))
+        h_mx_pool = stack.enter_context(tc.tile_pool(name="h_mx", bufs=2 * GROUPS))
         out_pool = stack.enter_context(tc.tile_pool(name="out", bufs=3))
         psum_z = stack.enter_context(tc.psum_pool(name="psum_z", bufs=1))
         psum_u = stack.enter_context(tc.psum_pool(name="psum_u", bufs=4))
@@ -79,6 +79,15 @@ def tile_mlpmodelpredictor_pb_t_kernel(tc, z2, sw1, b2, w3, b3, out):
             )
             z_raw[n] = rows
 
+        def load_s(col_half):
+            for u in range(PAIR):
+                nc.sync.dma_start(
+                    out=s_rows[:, col_half, PAIR * u : PAIR * (u + 1), :],
+                    in_=sw1[
+                        PAIR * P * u : PAIR * P * (u + 1), col_half * UNIT : (col_half + 1) * UNIT
+                    ].rearrange("(q e) c -> q e c", e=PAIR),
+                )
+
         def load_w(b):
             rows = w_pool.tile([P, CHUNKS, O], BF16, name="w_rows")
             nc.sync.dma_start(out=rows[:], in_=w3[b].rearrange("(c p) o -> p c o", p=P))
@@ -86,9 +95,9 @@ def tile_mlpmodelpredictor_pb_t_kernel(tc, z2, sw1, b2, w3, b3, out):
 
         def transpose_z(n):
             words = z_raw[n][:].bitcast(F32)
-            for half in range(2):
-                bank = psum_z.tile([P, 2, HALF], F32, name="z_bank%d" % half)
-                for u in range(2):
+            for half in range(UNIT // HALF):
+                bank = psum_z.tile([P, PAIR, HALF], F32, name="z_bank%d" % half)
+                for u in range(PAIR):
                     for i in range(HALF // P):
                         j = half * (HALF // P) + i
                         nc.tensor.transpose(
@@ -140,7 +149,7 @@ def tile_mlpmodelpredictor_pb_t_kernel(tc, z2, sw1, b2, w3, b3, out):
 
         def regroup_h(n, g):
             grouped = h_pool.tile([P, UNIT, PACK], BF16, name="h_grouped", align_bytes=64)
-            regroup(nc.vector.tensor_copy, grouped[:], planes[n, g][:])
+            regroup(nc, grouped[:], planes[n, g][:])
             h_grouped[n, g] = grouped
 
         def quantise_h(n, g):
@@ -153,7 +162,7 @@ def tile_mlpmodelpredictor_pb_t_kernel(tc, z2, sw1, b2, w3, b3, out):
             grouped = w_pool.tile([P, GROUPS * O, PACK], BF16, name="w_grouped", align_bytes=64)
             for g in range(GROUPS):
                 regroup(
-                    nc.vector.tensor_copy,
+                    nc,
                     grouped[:, g * O : (g + 1) * O, :],
                     w_raw[b][:, g * PACK : (g + 1) * PACK, :],
                 )
@@ -202,16 +211,6 @@ def tile_mlpmodelpredictor_pb_t_kernel(tc, z2, sw1, b2, w3, b3, out):
         b2_rows = keep.tile([P, P], BF16, name="b2_rows")
         b3_all = keep.tile([P, B, O], BF16, name="b3_all")
         nc.vector.memset(b2_rows[:], 0.0)
-
-        def load_s(col_half):
-            for u in range(2):
-                nc.sync.dma_start(
-                    out=s_rows[:, col_half, 2 * u : 2 * u + 2, :],
-                    in_=sw1[
-                        256 * u : 256 * (u + 1), col_half * UNIT : (col_half + 1) * UNIT
-                    ].rearrange("(q e) c -> q e c", e=2),
-                )
-
         nc.sync.dma_start(
             out=b2_rows[0 : B * CHUNKS, :], in_=b2.rearrange("b (c p) -> (b c) p", p=P)
         )
@@ -221,25 +220,14 @@ def tile_mlpmodelpredictor_pb_t_kernel(tc, z2, sw1, b2, w3, b3, out):
         load_s(1)
         load_z(2)
         load_w(0)
+        load_z(3)
         nc.sync.dma_start(
             out=b3_all[:].rearrange("p b o -> p (b o)"),
             in_=b3.rearrange("b o -> (b o)").partition_broadcast(P),
         )
-        load_z(3)
 
         ident = keep.tile([P, P], F32, name="ident")
         make_identity(nc, ident[:])
-
-        s_grouped = keep.tile([P, 2, UNIT, PACK], BF16, name="s_grouped", align_bytes=64)
-        s_codes = keep.tile([P, H], U32, name="s_codes", align_bytes=64)
-        s_scales = keep.tile([P, H], U8, name="s_scales", align_bytes=64)
-
-        def regroup_s(col_half):
-            regroup(nc.vector.tensor_copy, s_grouped[:, col_half], s_rows[:, col_half])
-
-        def quantise_s(col_half):
-            cols = slice(col_half * UNIT, (col_half + 1) * UNIT)
-            quantise(nc, s_codes[:, cols], s_scales[:, cols], s_grouped[:, col_half])
 
         b2_rows_f32 = keep.tile([P, P], F32, name="b2_rows_f32")
         nc.vector.tensor_copy(out=b2_rows_f32[:], in_=b2_rows[:])
@@ -247,6 +235,17 @@ def tile_mlpmodelpredictor_pb_t_kernel(tc, z2, sw1, b2, w3, b3, out):
         nc.tensor.transpose(out=b2_bank[:, 0, :], in_=b2_rows_f32[:], identity=ident[:])
         b2_cols = keep.tile([P, B * CHUNKS], F32, name="b2_cols")
         nc.vector.tensor_copy(out=b2_cols[:], in_=b2_bank[:, 0, 0 : B * CHUNKS])
+
+        s_grouped = keep.tile([P, 2, UNIT, PACK], BF16, name="s_grouped", align_bytes=64)
+        s_codes = keep.tile([P, H], U32, name="s_codes", align_bytes=64)
+        s_scales = keep.tile([P, H], U8, name="s_scales", align_bytes=64)
+
+        def regroup_s(col_half):
+            regroup(nc, s_grouped[:, col_half], s_rows[:, col_half])
+
+        def quantise_s(col_half):
+            cols = slice(col_half * UNIT, (col_half + 1) * UNIT)
+            quantise(nc, s_codes[:, cols], s_scales[:, cols], s_grouped[:, col_half])
 
         regroup_s(0)
         transpose_z(0)
@@ -260,36 +259,39 @@ def tile_mlpmodelpredictor_pb_t_kernel(tc, z2, sw1, b2, w3, b3, out):
         quantise_s(1)
         copy_z(1, 1, nc.vector.tensor_copy)
 
+        def live(n):
+            return 0 <= n < UNITS
+
         for n in range(UNITS + 2):
-            b, first_of_dataset = n // UNITS_PER_DATASET, n % UNITS_PER_DATASET == 0
-            if n + AHEAD < UNITS:
+            b = n // UNITS_PER_DATASET
+            new_dataset = live(n) and n % UNITS_PER_DATASET == 0
+            if live(n + AHEAD):
                 load_z(n + AHEAD)
-            if first_of_dataset and b + 1 < B:
+            if new_dataset and b + 1 < B:
                 load_w(b + 1)
-            if 1 <= n <= UNITS:
+            if live(n - 1):
                 regroup_h(n - 1, 1)
-            if n + 1 < UNITS:
+            if live(n + 1):
                 quantise_z(n + 1)
-            if n < UNITS:
+            if live(n):
                 hidden(n, 0)
-            if 1 <= n <= UNITS:
+            if live(n - 1):
                 quantise_h(n - 1, 1)
-            if n + 2 < UNITS:
-                vector_helps = n % VECTOR_EVERY == 0
+            if live(n + 2):
                 transpose_z(n + 2)
                 copy_z(n + 2, 0, nc.scalar.copy)
-                copy_z(n + 2, 1, nc.vector.tensor_copy if vector_helps else nc.scalar.copy)
-            if n < UNITS:
+                copy_z(n + 2, 1, nc.scalar.copy if new_dataset else nc.vector.tensor_copy)
+            if live(n):
                 hidden(n, 1)
-            if 1 <= n <= UNITS:
+            if live(n - 1):
                 output(n - 1)
-            if n < UNITS:
+            if live(n):
                 regroup_h(n, 0)
-                if first_of_dataset:
-                    regroup_w(b)
-            if n >= 2:
+            if new_dataset:
+                regroup_w(b)
+            if live(n - 2):
                 store(n - 2)
-            if n < UNITS:
+            if live(n):
                 quantise_h(n, 0)
-                if first_of_dataset:
-                    quantise_w(b)
+            if new_dataset:
+                quantise_w(b)

from contextlib import ExitStack

import concourse.mybir as mybir
from concourse.masks import make_identity

F32 = mybir.dt.float32
BF16 = mybir.dt.bfloat16
U32 = mybir.dt.uint32
U8 = mybir.dt.uint8
FP8X4 = mybir.dt.float8_e4m3fn_x4
RELU = mybir.ActivationFunctionType.Relu
ADD = mybir.AluOpType.add

T, B, R, H, O = 1024, 8, 512, 1024, 128
P = 128
PACK = 4
UNIT = 512
UNITS_PER_DATASET = T // UNIT
UNITS = B * UNITS_PER_DATASET
TOKEN_TILES = UNIT // P
CHUNKS = H // P
GROUPS = CHUNKS // PACK
HALF = UNIT // 2
PAIR = 2
AHEAD = 4

FLOPS = 2 * T * B * R * H + 2 * T * B * H * O


def regroup(nc, grouped, planes):
    nc.vector.tensor_copy(
        out=grouped.rearrange("p (c i) t -> p c t i", i=4),
        in_=planes.rearrange("p t (c i) -> p c t i", i=4),
    )


def quantise(nc, codes, scales, grouped):
    nc.vector.quantize_mx(
        out=codes.bitcast(FP8X4),
        scales=scales,
        in_=grouped.rearrange("p c t -> p (c t)"),
    )


def tile_mlpmodelpredictor_pb_t_kernel(tc, z2, sw1, b2, w3, b3, out):
    nc = tc.nc
    with ExitStack() as stack:
        keep = stack.enter_context(tc.tile_pool(name="keep", bufs=1))
        z_raw_pool = stack.enter_context(tc.tile_pool(name="z_raw", bufs=AHEAD))
        w_pool = stack.enter_context(tc.tile_pool(name="w3", bufs=2))
        z_pool = stack.enter_context(tc.tile_pool(name="z", bufs=2))
        plane_pool = stack.enter_context(tc.tile_pool(name="planes", bufs=3))
        h_pool = stack.enter_context(tc.tile_pool(name="h", bufs=2))
        h_mx_pool = stack.enter_context(tc.tile_pool(name="h_mx", bufs=2 * GROUPS))
        out_pool = stack.enter_context(tc.tile_pool(name="out", bufs=3))
        psum_z = stack.enter_context(tc.psum_pool(name="psum_z", bufs=1))
        psum_u = stack.enter_context(tc.psum_pool(name="psum_u", bufs=4))
        psum_o = stack.enter_context(tc.psum_pool(name="psum_o", bufs=2))
        stack.enter_context(tc.manual_schedule())

        z_raw = {}
        z_banks = {}
        z_grouped = {}
        z_mx = {}
        planes = {}
        h_grouped = {}
        h_mx = {}
        w_raw = {}
        w_grouped = {}
        w_mx = {}
        o_banks = {}

        def load_z(n):
            b, s = divmod(n, UNITS_PER_DATASET)
            rows = z_raw_pool.tile([P, TOKEN_TILES, R], BF16, name="z_rows")
            nc.sync.dma_start(
                out=rows[:],
                in_=z2[s * UNIT : (s + 1) * UNIT, b, :].rearrange("(j p) r -> p j r", p=P),
            )
            z_raw[n] = rows

        def load_s(col_half):
            for u in range(PAIR):
                nc.sync.dma_start(
                    out=s_rows[:, col_half, PAIR * u : PAIR * (u + 1), :],
                    in_=sw1[
                        PAIR * P * u : PAIR * P * (u + 1), col_half * UNIT : (col_half + 1) * UNIT
                    ].rearrange("(q e) c -> q e c", e=PAIR),
                )

        def load_w(b):
            rows = w_pool.tile([P, CHUNKS, O], BF16, name="w_rows")
            nc.sync.dma_start(out=rows[:], in_=w3[b].rearrange("(c p) o -> p c o", p=P))
            w_raw[b] = rows

        def transpose_z(n):
            words = z_raw[n][:].bitcast(F32)
            for half in range(UNIT // HALF):
                bank = psum_z.tile([P, PAIR, HALF], F32, name="z_bank%d" % half)
                for u in range(PAIR):
                    for i in range(HALF // P):
                        j = half * (HALF // P) + i
                        nc.tensor.transpose(
                            out=bank[:, u, i * P : (i + 1) * P],
                            in_=words[:, j, u * P : (u + 1) * P],
                            identity=ident[:],
                        )
                z_banks[n, half] = bank

        def copy_z(n, half, copy):
            if half == 0:
                z_grouped[n] = z_pool.tile([P, UNIT, PACK], BF16, name="z_grouped", align_bytes=64)
            copy(
                out=z_grouped[n][:].bitcast(F32)[:, half * HALF : (half + 1) * HALF, :],
                in_=z_banks[n, half][:].rearrange("p u r -> p r u"),
            )

        def quantise_z(n):
            codes = z_pool.tile([P, UNIT], U32, name="z_codes", align_bytes=64)
            scales = z_pool.tile([P, UNIT], U8, name="z_scales", align_bytes=64)
            quantise(nc, codes[:], scales[:], z_grouped[n][:])
            z_mx[n] = (codes, scales)

        def hidden(n, g):
            b = n // UNITS_PER_DATASET
            z_codes, z_scales = z_mx[n]
            four = plane_pool.tile([P, PACK, UNIT], BF16, name="planes")
            for t in range(PACK):
                c = g * PACK + t
                cols = slice(c * P, (c + 1) * P)
                u_bank = psum_u.tile([P, UNIT], F32, name="u_bank")
                nc.tensor.matmul_mx(
                    out=u_bank[:],
                    lhsT=s_codes[:, cols].bitcast(FP8X4),
                    lhsT_scale=s_scales[:, cols],
                    rhs=z_codes[:].bitcast(FP8X4),
                    rhs_scale=z_scales[:],
                    start=True,
                    stop=True,
                )
                nc.scalar.activation(
                    out=four[:, t, :],
                    in_=u_bank[:],
                    func=RELU,
                    bias=b2_cols[:, b * CHUNKS + c : b * CHUNKS + c + 1],
                    scale=1.0,
                )
            planes[n, g] = four

        def regroup_h(n, g):
            grouped = h_pool.tile([P, UNIT, PACK], BF16, name="h_grouped", align_bytes=64)
            regroup(nc, grouped[:], planes[n, g][:])
            h_grouped[n, g] = grouped

        def quantise_h(n, g):
            codes = h_mx_pool.tile([P, UNIT], U32, name="h_codes", align_bytes=64)
            scales = h_mx_pool.tile([P, UNIT], U8, name="h_scales", align_bytes=64)
            quantise(nc, codes[:], scales[:], h_grouped[n, g][:])
            h_mx[n, g] = (codes, scales)

        def regroup_w(b):
            grouped = w_pool.tile([P, GROUPS * O, PACK], BF16, name="w_grouped", align_bytes=64)
            for g in range(GROUPS):
                regroup(
                    nc,
                    grouped[:, g * O : (g + 1) * O, :],
                    w_raw[b][:, g * PACK : (g + 1) * PACK, :],
                )
            w_grouped[b] = grouped

        def quantise_w(b):
            codes = w_pool.tile([P, GROUPS * O], U32, name="w_codes", align_bytes=64)
            scales = w_pool.tile([P, GROUPS * O], U8, name="w_scales", align_bytes=64)
            quantise(nc, codes[:], scales[:], w_grouped[b][:])
            w_mx[b] = (codes, scales)

        def output(n):
            w_codes, w_scales = w_mx[n // UNITS_PER_DATASET]
            o_bank = psum_o.tile([P, TOKEN_TILES, O], F32, name="o_bank")
            for j in range(TOKEN_TILES):
                tokens = slice(j * P, (j + 1) * P)
                for g in range(GROUPS):
                    h_codes, h_scales = h_mx[n, g]
                    w_cols = slice(g * O, (g + 1) * O)
                    nc.tensor.matmul_mx(
                        out=o_bank[:, j, :],
                        lhsT=h_codes[:, tokens].bitcast(FP8X4),
                        lhsT_scale=h_scales[:, tokens],
                        rhs=w_codes[:, w_cols].bitcast(FP8X4),
                        rhs_scale=w_scales[:, w_cols],
                        start=(g == 0),
                        stop=(g == GROUPS - 1),
                    )
            o_banks[n] = o_bank

        def store(n):
            b, s = divmod(n, UNITS_PER_DATASET)
            result = out_pool.tile([P, TOKEN_TILES, O], F32, name="result")
            nc.vector.tensor_tensor(
                out=result[:],
                in0=o_banks[n][:],
                in1=b3_all[:, b, :].unsqueeze(1).to_broadcast([P, TOKEN_TILES, O]),
                op=ADD,
            )
            nc.sync.dma_start(
                out=out[s * UNIT : (s + 1) * UNIT, b, :].rearrange("(j p) o -> p j o", p=P),
                in_=result[:],
            )

        s_rows = keep.tile([P, 2, PACK, UNIT], BF16, name="s_rows")
        b2_rows = keep.tile([P, P], BF16, name="b2_rows")
        b3_all = keep.tile([P, B, O], BF16, name="b3_all")
        nc.vector.memset(b2_rows[:], 0.0)
        nc.sync.dma_start(
            out=b2_rows[0 : B * CHUNKS, :], in_=b2.rearrange("b (c p) -> (b c) p", p=P)
        )
        load_s(0)
        load_z(0)
        load_z(1)
        load_s(1)
        load_z(2)
        load_w(0)
        load_z(3)
        nc.sync.dma_start(
            out=b3_all[:].rearrange("p b o -> p (b o)"),
            in_=b3.rearrange("b o -> (b o)").partition_broadcast(P),
        )

        ident = keep.tile([P, P], F32, name="ident")
        make_identity(nc, ident[:])

        b2_rows_f32 = keep.tile([P, P], F32, name="b2_rows_f32")
        nc.vector.tensor_copy(out=b2_rows_f32[:], in_=b2_rows[:])
        b2_bank = psum_o.tile([P, TOKEN_TILES, O], F32, name="o_bank")
        nc.tensor.transpose(out=b2_bank[:, 0, :], in_=b2_rows_f32[:], identity=ident[:])
        b2_cols = keep.tile([P, B * CHUNKS], F32, name="b2_cols")
        nc.vector.tensor_copy(out=b2_cols[:], in_=b2_bank[:, 0, 0 : B * CHUNKS])

        s_grouped = keep.tile([P, 2, UNIT, PACK], BF16, name="s_grouped", align_bytes=64)
        s_codes = keep.tile([P, H], U32, name="s_codes", align_bytes=64)
        s_scales = keep.tile([P, H], U8, name="s_scales", align_bytes=64)

        def regroup_s(col_half):
            regroup(nc, s_grouped[:, col_half], s_rows[:, col_half])

        def quantise_s(col_half):
            cols = slice(col_half * UNIT, (col_half + 1) * UNIT)
            quantise(nc, s_codes[:, cols], s_scales[:, cols], s_grouped[:, col_half])

        regroup_s(0)
        transpose_z(0)
        quantise_s(0)
        copy_z(0, 0, nc.scalar.copy)
        copy_z(0, 1, nc.vector.tensor_copy)
        quantise_z(0)
        transpose_z(1)
        regroup_s(1)
        copy_z(1, 0, nc.vector.tensor_copy)
        quantise_s(1)
        copy_z(1, 1, nc.vector.tensor_copy)

        def live(n):
            return 0 <= n < UNITS

        for n in range(UNITS + 2):
            b = n // UNITS_PER_DATASET
            new_dataset = live(n) and n % UNITS_PER_DATASET == 0
            if live(n + AHEAD):
                load_z(n + AHEAD)
            if new_dataset and b + 1 < B:
                load_w(b + 1)
            if live(n - 1):
                regroup_h(n - 1, 1)
            if live(n + 1):
                quantise_z(n + 1)
            if live(n):
                hidden(n, 0)
            if live(n - 1):
                quantise_h(n - 1, 1)
            if live(n + 2):
                transpose_z(n + 2)
                copy_z(n + 2, 0, nc.scalar.copy)
                copy_z(n + 2, 1, nc.scalar.copy if new_dataset else nc.vector.tensor_copy)
            if live(n):
                hidden(n, 1)
            if live(n - 1):
                output(n - 1)
            if live(n):
                regroup_h(n, 0)
            if new_dataset:
                regroup_w(b)
            if live(n - 2):
                store(n - 2)
            if live(n):
                quantise_h(n, 0)
            if new_dataset:
                quantise_w(b)
